import numpy as np
import ml_dtypes


def mxq(x, axis, fmt="e4m3"):
    dtype, down = {"e4m3": (ml_dtypes.float8_e4m3fn, 7), "e5m2": (ml_dtypes.float8_e5m2, 14)}[fmt]
    v = np.moveaxis(np.asarray(x, np.float32).astype(ml_dtypes.bfloat16).astype(np.float64), axis, -1)
    blocks = v.reshape(v.shape[:-1] + (-1, 32))
    amax = np.abs(blocks).max(-1, keepdims=True)
    byte = np.maximum(np.where(amax > 0, np.frexp(amax)[1] - 1 + 127, 0) - down, 1)
    scale = np.exp2(byte - 127.0)
    codes = (blocks / scale).astype(np.float32).astype(dtype).astype(np.float64)
    return np.moveaxis((codes * scale).reshape(v.shape), -1, axis)


WIDE = False


def mx_kscale(k):
    if not WIDE:
        return np.ones(k)
    levels = np.array([10, -10, 5, -5, 0])
    a = np.random.permutation(np.resize(levels, k // 512 * 4)).reshape(k // 512, 4)
    idx = np.arange(k)
    return np.exp2(a[idx // 512, idx % 128 // 32])


BF16 = ml_dtypes.bfloat16


def bf(x):
    return np.asarray(x, np.float32).astype(BF16)


def f64(x):
    return np.asarray(x).astype(np.float64)


B, S, D, H, DH, F = 2, 128, 2048, 16, 128, 4096
E = H * DH
EPS = 1e-5
NTERMS = 120


def layernorm(x, g, b):
    mu = x.mean(-1, keepdims=True)
    var = np.square(x - mu).mean(-1, keepdims=True)
    return (x - mu) / np.sqrt(var + EPS) * g + b


def erf(v):
    a = np.minimum(np.maximum(v, -6.0), 6.0)
    term = a.copy()
    total = a.copy()
    for n in range(1, NTERMS):
        term = term * (2.0 * a * a) / (2.0 * n + 1.0)
        total = total + term
    return 2.0 / np.sqrt(np.pi) * np.exp(-a * a) * total


def gelu_erf(v):
    return 0.5 * v * (1.0 + erf(v / np.sqrt(2.0)))


def setup_inputs():
    s, t = mx_kscale(E), mx_kscale(D)
    x = np.random.standard_normal((B, S, D)) + 0.5 * np.random.standard_normal((B, S, 1))
    return {"h_attn": bf(0.2 * np.random.standard_normal((B, S, E)) * s),
            "x": bf(x),
            "w_out": bf(np.random.standard_normal((D, E)) * 2.0 / np.sqrt(E) / s),
            "w_fc1": bf(np.random.standard_normal((F, D)) / np.sqrt(D) / t),
            "g2": bf((1.0 + 0.1 * np.random.standard_normal(D)) * t),
            "b2": bf(0.1 * np.random.standard_normal(D) * t)}


def reference(h_attn, x, w_out, w_fc1, g2, b2):
    x_mid = f64(x) + (mxq(f64(h_attn), 2, "e4m3") @ mxq(f64(w_out), 1, "e4m3").T)
    h = layernorm(x_mid, f64(g2), f64(b2))
    u = mxq(h, 2, "e4m3") @ mxq(f64(w_fc1), 1, "e4m3").T
    return x_mid, gelu_erf(u)

@@ -1,0 +1,237 @@
+from contextlib import ExitStack
+
+import concourse.mybir as mybir
+from concourse.masks import make_identity
+
+F32 = mybir.dt.float32
+BF16 = mybir.dt.bfloat16
+U32 = mybir.dt.uint32
+U8 = mybir.dt.uint8
+FP8X4 = mybir.dt.float8_e4m3fn_x4
+ACT = mybir.ActivationFunctionType
+ALU = mybir.AluOpType
+
+P = 128
+PACK = 4
+K = 2048
+PASSES = K // (P * PACK)
+TOKENS = 256
+TOKEN_TILES = TOKENS // P
+D_MODEL = 2048
+D_FF = 4096
+BLOCK = 256
+GROUP = 512
+GROUPS_OUT = D_MODEL // GROUP
+GROUPS = GROUPS_OUT + D_FF // GROUP
+EPS = 1e-5
+
+RAW_BUFS = 10
+FIRST_SHARED_GROUP = 7
+
+FLOPS = 2 * TOKENS * K * (D_MODEL + D_FF)
+
+
+def tile_minitransformerlayer_pb_kernel(tc, h_attn, x, w_out, w_fc1, g2, b2, out_0, out_1):
+    nc = tc.nc
+    x_rows = x.flatten_outer_dims()
+    x_mid_rows = out_0.flatten_outer_dims()
+    act_rows = out_1.flatten_outer_dims()
+
+    blocks = [h_attn.flatten_outer_dims()]
+    blocks.extend([w_out[r : r + BLOCK, :] for r in range(0, D_MODEL, BLOCK)])
+    blocks.extend([w_fc1[r : r + BLOCK, :] for r in range(0, D_FF, BLOCK)])
+
+    with ExitStack() as ctx:
+        ctx.enter_context(tc.manual_schedule())
+        const = ctx.enter_context(tc.tile_pool(name="const", bufs=1))
+        raw_pool = ctx.enter_context(tc.tile_pool(name="raw", bufs=RAW_BUFS))
+        grouped_pool = ctx.enter_context(tc.tile_pool(name="grouped", bufs=6))
+        weight_pool = ctx.enter_context(tc.tile_pool(name="weights", bufs=4))
+        result_pool = ctx.enter_context(tc.tile_pool(name="result", bufs=4))
+        bank_pool = ctx.enter_context(tc.psum_pool(name="banks", bufs=6))
+        acc_pool = ctx.enter_context(tc.psum_pool(name="acc", bufs=2))
+
+        zero = const.tile([P, 1], F32)
+        nc.vector.memset(zero[:], 0.0)
+        table_warmer = const.tile([P, 1], F32)
+        nc.scalar.activation(out=table_warmer[:], in_=zero[:], func=ACT.Gelu)
+
+        ident = const.tile([P, P], F32)
+        make_identity(nc, ident[:])
+        minus_half = const.tile([P, TOKEN_TILES], F32)
+        nc.gpsimd.memset(minus_half[:], -0.5)
+
+        loaded = []
+
+        def load_next_block():
+            if len(loaded) < len(blocks):
+                raw = raw_pool.tile([P, 2, K], BF16)
+                rows = blocks[len(loaded)]
+                nc.sync.dma_start(out=raw[:], in_=rows.rearrange("(p c) k -> p c k", c=2))
+                loaded.append(raw)
+
+        gain_rows = const.tile([P, 2 * P], BF16)
+        nc.vector.memset(gain_rows[:], 0.0)
+        nc.scalar.dma_start(out=gain_rows[0:8, :], in_=g2.rearrange("(r c) -> r c", c=2 * P))
+        nc.scalar.dma_start(out=gain_rows[8:16, :], in_=b2.rearrange("(r c) -> r c", c=2 * P))
+
+        x_sb = const.tile([P, TOKEN_TILES, D_MODEL], BF16)
+        for b in range(RAW_BUFS):
+            load_next_block()
+            if b == 2:
+                nc.sync.dma_start(out=x_sb[:], in_=x_rows.rearrange("(t p) d -> p t d", p=P))
+
+        def quantise(grouped, codes, scales):
+            nc.vector.quantize_mx(
+                out=codes.bitcast(FP8X4),
+                scales=scales,
+                in_=grouped[:].rearrange("p n t -> p (n t)"),
+            )
+
+        def pack_block(b, codes, scales, vector_every):
+            words = loaded[b][:].bitcast(F32)
+            waiting = None
+            for g in range(PASSES):
+                bank = bank_pool.tile([P, 2, 2, P], F32)
+                for u in range(2):
+                    first = (2 * g + u) * P
+                    for c in range(2):
+                        nc.tensor.transpose(bank[:, u, c, :], words[:, c, first : first + P], ident[:])
+                grouped = grouped_pool.tile([P, BLOCK, PACK], BF16, align_bytes=64)
+                to_words = grouped[:].bitcast(F32).rearrange("p (j c) u -> p j c u", c=2)
+                from_bank = bank[:].rearrange("p u c j -> p j c u")
+                bank_number = b * PASSES + g
+                if vector_every and bank_number % vector_every == vector_every - 1:
+                    nc.vector.tensor_copy(out=to_words, in_=from_bank)
+                else:
+                    nc.scalar.copy(out=to_words, in_=from_bank)
+                if waiting is not None:
+                    quantise(*waiting)
+                waiting = (grouped, codes[:, g, :], scales[:, g, :])
+            quantise(*waiting)
+            load_next_block()
+
+        def prepare_group(i):
+            codes = weight_pool.tile([P, PASSES, GROUP], U32, align_bytes=64)
+            scales = weight_pool.tile([P, PASSES, GROUP], U8, align_bytes=64)
+            for half in range(2):
+                cols = slice(half * BLOCK, (half + 1) * BLOCK)
+                pack_block(
+                    1 + 2 * i + half,
+                    codes[:, :, cols],
+                    scales[:, :, cols],
+                    3 if i >= FIRST_SHARED_GROUP else 0,
+                )
+            return codes, scales
+
+        def mx_product(tokens, weights, tt):
+            token_codes, token_scales = tokens
+            weight_codes, weight_scales = weights
+            rows = slice(tt * P, (tt + 1) * P)
+            acc = acc_pool.tile([P, GROUP], F32)
+            for g in range(PASSES):
+                nc.tensor.matmul_mx(
+                    out=acc[:],
+                    lhsT=token_codes[:, g, rows].bitcast(FP8X4),
+                    lhsT_scale=token_scales[:, g, rows],
+                    rhs=weight_codes[:, g, :].bitcast(FP8X4),
+                    rhs_scale=weight_scales[:, g, :],
+                    start=(g == 0),
+                    stop=(g == PASSES - 1),
+                )
+            return acc
+
+        attn_codes = const.tile([P, PASSES, TOKENS], U32, align_bytes=64)
+        attn_scales = const.tile([P, PASSES, TOKENS], U8, align_bytes=64)
+        x_mid = const.tile([P, TOKEN_TILES, D_MODEL], F32)
+        stats = const.tile([P, TOKEN_TILES, GROUPS_OUT, 6], F32)
+
+        def project_group(i, weights):
+            cols = slice(i * GROUP, (i + 1) * GROUP)
+            for tt in range(TOKEN_TILES):
+                acc = mx_product((attn_codes, attn_scales), weights, tt)
+                nc.vector.tensor_tensor(out=x_mid[:, tt, cols], in0=acc[:], in1=x_sb[:, tt, cols], op=ALU.add)
+                nc.vector.bn_stats(out=stats[:, tt, i, :], in_=x_mid[:, tt, cols])
+
+        pack_block(0, attn_codes[:], attn_scales[:], 2)
+
+        bank = bank_pool.tile([P, 2, 2, P], F32)
+        nc.tensor.transpose(bank[:, 0, 0, :], gain_rows[:].bitcast(F32), ident[:])
+        gain_words = const.tile([P, 16], F32)
+        nc.vector.tensor_copy(out=gain_words[:], in_=bank[:, 0, 0, 0:16])
+        gain_bias = const.tile([P, 16, 2], F32)
+        nc.vector.tensor_copy(out=gain_bias[:], in_=gain_words[:].bitcast(BF16).rearrange("p (r e) -> p r e", e=2))
+        gain = gain_bias[:, 0:8, :]
+        bias = gain_bias[:, 8:16, :]
+
+        prepared = {0: prepare_group(0)}
+        for i in range(1, GROUPS_OUT + 1):
+            prepared[i] = prepare_group(i)
+            project_group(i - 1, prepared[i - 1])
+        for tt in range(TOKEN_TILES):
+            nc.sync.dma_start(out=x_mid_rows[tt * P : (tt + 1) * P, :], in_=x_mid[:, tt, :])
+
+        mean_var = const.tile([P, TOKEN_TILES, 2], F32)
+        for tt in range(TOKEN_TILES):
+            nc.vector.bn_aggr(out=mean_var[:, tt, :], in_=stats[:, tt, :, :].rearrange("p i s -> p (i s)"))
+        var_eps = const.tile([P, TOKEN_TILES], F32)
+        nc.vector.tensor_scalar_add(out=var_eps[:], in0=mean_var[:, :, 1], scalar1=EPS)
+        rstd = const.tile([P, TOKEN_TILES], F32)
+        nc.gpsimd.tensor_tensor(out=rstd[:], in0=var_eps[:], in1=minus_half[:], op=ALU.pow)
+        z = const.tile([P, TOKEN_TILES, D_MODEL], F32)
+        for g in range(PASSES):
+            cols = slice(g * P * PACK, (g + 1) * P * PACK)
+            for tt in range(TOKEN_TILES):
+                nc.vector.tensor_scalar(
+                    out=z[:, tt, cols],
+                    in0=x_mid[:, tt, cols],
+                    scalar1=mean_var[:, tt, 0:1],
+                    scalar2=rstd[:, tt : tt + 1],
+                    op0=ALU.subtract,
+                    op1=ALU.mult,
+                )
+
+        prepared[5] = prepare_group(5)
+
+        h_codes = const.tile([P, PASSES, TOKENS], U32, align_bytes=64)
+        h_scales = const.tile([P, PASSES, TOKENS], U8, align_bytes=64)
+        h_planes = const.tile([P, PASSES, PACK, TOKENS], BF16)
+        z_by_parity = z[:].rearrange("p t (q e) -> p t e q", e=2)
+        for g in range(PASSES):
+            for u in range(2):
+                bank = bank_pool.tile([P, 2, 2, P], F32)
+                first = (2 * g + u) * P
+                for e in range(2):
+                    for tt in range(TOKEN_TILES):
+                        nc.tensor.transpose(bank[:, e, tt, :], z_by_parity[:, tt, e, first : first + P], ident[:])
+                for e in range(2):
+                    plane = h_planes[:, g, 2 * u + e, :]
+                    z_t = bank[:, e, :, :].rearrange("p t j -> p (t j)")
+                    scale_ap = gain[:, 2 * g + u, e : e + 1]
+                    bias_ap = bias[:, 2 * g + u, e : e + 1]
+                    if u == 0:
+                        nc.scalar.activation(out=plane, in_=z_t, func=ACT.Identity, bias=bias_ap, scale=scale_ap)
+                    else:
+                        nc.vector.tensor_scalar(
+                            out=plane, in0=z_t, scalar1=scale_ap, scalar2=bias_ap, op0=ALU.mult, op1=ALU.add
+                        )
+            grouped = grouped_pool.tile([P, BLOCK, PACK], BF16, align_bytes=64)
+            nc.vector.tensor_copy(out=grouped[:], in_=h_planes[:, g, :, :].rearrange("p t n -> p n t"))
+            quantise(grouped, h_codes[:, g, :], h_scales[:, g, :])
+
+        prepared[6] = prepare_group(6)
+
+        def mlp_group(i, weights):
+            cols = slice((i - GROUPS_OUT) * GROUP, (i - GROUPS_OUT + 1) * GROUP)
+            for tt in range(TOKEN_TILES):
+                acc = mx_product((h_codes, h_scales), weights, tt)
+                result = result_pool.tile([P, GROUP], F32)
+                nc.scalar.activation(out=result[:], in_=acc[:], func=ACT.Gelu)
+                nc.sync.dma_start(out=act_rows[tt * P : (tt + 1) * P, cols], in_=result[:])
+
+        mlp_group(4, prepared[4])
+        mlp_group(5, prepared[5])
+        for i in range(7, GROUPS):
+            prepared[i] = prepare_group(i)
+            mlp_group(i - 1, prepared[i - 1])
+        mlp_group(GROUPS - 1, prepared[GROUPS - 1])

@@ -45,9 +45,9 @@ def tile_minitransformerlayer_pb_kernel(tc, h_attn, x, w_out, w_fc1, g2, b2, out
         ctx.enter_context(tc.manual_schedule())
         const = ctx.enter_context(tc.tile_pool(name="const", bufs=1))
         raw_pool = ctx.enter_context(tc.tile_pool(name="raw", bufs=RAW_BUFS))
-        grouped_pool = ctx.enter_context(tc.tile_pool(name="grouped", bufs=6))
+        grouped_pool = ctx.enter_context(tc.tile_pool(name="grouped", bufs=10))
         weight_pool = ctx.enter_context(tc.tile_pool(name="weights", bufs=4))
-        result_pool = ctx.enter_context(tc.tile_pool(name="result", bufs=4))
+        result_pool = ctx.enter_context(tc.tile_pool(name="result", bufs=8))
         bank_pool = ctx.enter_context(tc.psum_pool(name="banks", bufs=6))
         acc_pool = ctx.enter_context(tc.psum_pool(name="acc", bufs=2))
 
@@ -78,7 +78,7 @@ def tile_minitransformerlayer_pb_kernel(tc, h_attn, x, w_out, w_fc1, g2, b2, out
         x_sb = const.tile([P, TOKEN_TILES, D_MODEL], BF16)
         for b in range(RAW_BUFS):
             load_next_block()
-            if b == 2:
+            if b == 4:
                 nc.sync.dma_start(out=x_sb[:], in_=x_rows.rearrange("(t p) d -> p t d", p=P))
 
         def quantise(grouped, codes, scales):
@@ -88,7 +88,7 @@ def tile_minitransformerlayer_pb_kernel(tc, h_attn, x, w_out, w_fc1, g2, b2, out
                 in_=grouped[:].rearrange("p n t -> p (n t)"),
             )
 
-        def pack_block(b, codes, scales, vector_every):
+        def pack_block(b, codes, scales, vector_every, postponed=None):
             words = loaded[b][:].bitcast(F32)
             waiting = None
             for g in range(PASSES):
@@ -105,13 +105,17 @@ def tile_minitransformerlayer_pb_kernel(tc, h_attn, x, w_out, w_fc1, g2, b2, out
                     nc.vector.tensor_copy(out=to_words, in_=from_bank)
                 else:
                     nc.scalar.copy(out=to_words, in_=from_bank)
+                if postponed is not None:
+                    postponed.append((grouped, codes[:, g, :], scales[:, g, :]))
+                    continue
                 if waiting is not None:
                     quantise(*waiting)
                 waiting = (grouped, codes[:, g, :], scales[:, g, :])
-            quantise(*waiting)
+            if waiting is not None:
+                quantise(*waiting)
             load_next_block()
 
-        def prepare_group(i):
+        def prepare_group(i, postponed=None):
             codes = weight_pool.tile([P, PASSES, GROUP], U32, align_bytes=64)
             scales = weight_pool.tile([P, PASSES, GROUP], U8, align_bytes=64)
             for half in range(2):
@@ -121,6 +125,7 @@ def tile_minitransformerlayer_pb_kernel(tc, h_attn, x, w_out, w_fc1, g2, b2, out
                     codes[:, :, cols],
                     scales[:, :, cols],
                     3 if i >= FIRST_SHARED_GROUP else 0,
+                    postponed,
                 )
             return codes, scales
 
@@ -165,9 +170,10 @@ def tile_minitransformerlayer_pb_kernel(tc, h_attn, x, w_out, w_fc1, g2, b2, out
         bias = gain_bias[:, 8:16, :]
 
         prepared = {0: prepare_group(0)}
-        for i in range(1, GROUPS_OUT + 1):
+        for i in range(1, GROUPS_OUT):
             prepared[i] = prepare_group(i)
             project_group(i - 1, prepared[i - 1])
+        project_group(GROUPS_OUT - 1, prepared[GROUPS_OUT - 1])
         for tt in range(TOKEN_TILES):
             nc.sync.dma_start(out=x_mid_rows[tt * P : (tt + 1) * P, :], in_=x_mid[:, tt, :])
 
@@ -191,7 +197,8 @@ def tile_minitransformerlayer_pb_kernel(tc, h_attn, x, w_out, w_fc1, g2, b2, out
                     op1=ALU.mult,
                 )
 
-        prepared[5] = prepare_group(5)
+        postponed = []
+        prepared[4] = prepare_group(4, postponed)
 
         h_codes = const.tile([P, PASSES, TOKENS], U32, align_bytes=64)
         h_scales = const.tile([P, PASSES, TOKENS], U8, align_bytes=64)
@@ -209,17 +216,13 @@ def tile_minitransformerlayer_pb_kernel(tc, h_attn, x, w_out, w_fc1, g2, b2, out
                     z_t = bank[:, e, :, :].rearrange("p t j -> p (t j)")
                     scale_ap = gain[:, 2 * g + u, e : e + 1]
                     bias_ap = bias[:, 2 * g + u, e : e + 1]
-                    if u == 0:
-                        nc.scalar.activation(out=plane, in_=z_t, func=ACT.Identity, bias=bias_ap, scale=scale_ap)
-                    else:
-                        nc.vector.tensor_scalar(
-                            out=plane, in0=z_t, scalar1=scale_ap, scalar2=bias_ap, op0=ALU.mult, op1=ALU.add
-                        )
+                    nc.scalar.activation(out=plane, in_=z_t, func=ACT.Identity, bias=bias_ap, scale=scale_ap)
+            share = len(postponed) // PASSES
+            for arguments in postponed[g * share : (g + 1) * share]:
+                quantise(*arguments)
             grouped = grouped_pool.tile([P, BLOCK, PACK], BF16, align_bytes=64)
             nc.vector.tensor_copy(out=grouped[:], in_=h_planes[:, g, :, :].rearrange("p t n -> p n t"))
             quantise(grouped, h_codes[:, g, :], h_scales[:, g, :])
-
-        prepared[6] = prepare_group(6)
 
         def mlp_group(i, weights):
             cols = slice((i - GROUPS_OUT) * GROUP, (i - GROUPS_OUT + 1) * GROUP)
@@ -229,9 +232,7 @@ def tile_minitransformerlayer_pb_kernel(tc, h_attn, x, w_out, w_fc1, g2, b2, out
                 nc.scalar.activation(out=result[:], in_=acc[:], func=ACT.Gelu)
                 nc.sync.dma_start(out=act_rows[tt * P : (tt + 1) * P, cols], in_=result[:])
 
-        mlp_group(4, prepared[4])
-        mlp_group(5, prepared[5])
-        for i in range(7, GROUPS):
+        for i in range(GROUPS_OUT + 1, GROUPS):
             prepared[i] = prepare_group(i)
             mlp_group(i - 1, prepared[i - 1])
         mlp_group(GROUPS - 1, prepared[GROUPS - 1])

@@ -26,7 +26,6 @@ GROUPS = GROUPS_OUT + D_FF // GROUP
 EPS = 1e-5
 
 RAW_BUFS = 10
-FIRST_SHARED_GROUP = 7
 
 FLOPS = 2 * TOKENS * K * (D_MODEL + D_FF)
 
@@ -45,7 +44,7 @@ def tile_minitransformerlayer_pb_kernel(tc, h_attn, x, w_out, w_fc1, g2, b2, out
         ctx.enter_context(tc.manual_schedule())
         const = ctx.enter_context(tc.tile_pool(name="const", bufs=1))
         raw_pool = ctx.enter_context(tc.tile_pool(name="raw", bufs=RAW_BUFS))
-        grouped_pool = ctx.enter_context(tc.tile_pool(name="grouped", bufs=10))
+        grouped_pool = ctx.enter_context(tc.tile_pool(name="grouped", bufs=8))
         weight_pool = ctx.enter_context(tc.tile_pool(name="weights", bufs=4))
         result_pool = ctx.enter_context(tc.tile_pool(name="result", bufs=8))
         bank_pool = ctx.enter_context(tc.psum_pool(name="banks", bufs=6))
@@ -88,7 +87,7 @@ def tile_minitransformerlayer_pb_kernel(tc, h_attn, x, w_out, w_fc1, g2, b2, out
                 in_=grouped[:].rearrange("p n t -> p (n t)"),
             )
 
-        def pack_block(b, codes, scales, vector_every, postponed=None):
+        def pack_block(b, codes, scales, vector_every):
             words = loaded[b][:].bitcast(F32)
             waiting = None
             for g in range(PASSES):
@@ -105,28 +104,24 @@ def tile_minitransformerlayer_pb_kernel(tc, h_attn, x, w_out, w_fc1, g2, b2, out
                     nc.vector.tensor_copy(out=to_words, in_=from_bank)
                 else:
                     nc.scalar.copy(out=to_words, in_=from_bank)
-                if postponed is not None:
-                    postponed.append((grouped, codes[:, g, :], scales[:, g, :]))
-                    continue
                 if waiting is not None:
                     quantise(*waiting)
                 waiting = (grouped, codes[:, g, :], scales[:, g, :])
-            if waiting is not None:
-                quantise(*waiting)
+            quantise(*waiting)
             load_next_block()
 
-        def prepare_group(i, postponed=None):
+        def prepare_group(i):
+            if i < GROUPS_OUT:
+                vector_every = 4
+            elif i == GROUPS_OUT:
+                vector_every = 0
+            else:
+                vector_every = 3
             codes = weight_pool.tile([P, PASSES, GROUP], U32, align_bytes=64)
             scales = weight_pool.tile([P, PASSES, GROUP], U8, align_bytes=64)
             for half in range(2):
                 cols = slice(half * BLOCK, (half + 1) * BLOCK)
-                pack_block(
-                    1 + 2 * i + half,
-                    codes[:, :, cols],
-                    scales[:, :, cols],
-                    3 if i >= FIRST_SHARED_GROUP else 0,
-                    postponed,
-                )
+                pack_block(1 + 2 * i + half, codes[:, :, cols], scales[:, :, cols], vector_every)
             return codes, scales
 
         def mx_product(tokens, weights, tt):
@@ -197,8 +192,7 @@ def tile_minitransformerlayer_pb_kernel(tc, h_attn, x, w_out, w_fc1, g2, b2, out
                     op1=ALU.mult,
                 )
 
-        postponed = []
-        prepared[4] = prepare_group(4, postponed)
+        prepared[GROUPS_OUT] = prepare_group(GROUPS_OUT)
 
         h_codes = const.tile([P, PASSES, TOKENS], U32, align_bytes=64)
         h_scales = const.tile([P, PASSES, TOKENS], U8, align_bytes=64)
@@ -217,9 +211,6 @@ def tile_minitransformerlayer_pb_kernel(tc, h_attn, x, w_out, w_fc1, g2, b2, out
                     scale_ap = gain[:, 2 * g + u, e : e + 1]
                     bias_ap = bias[:, 2 * g + u, e : e + 1]
                     nc.scalar.activation(out=plane, in_=z_t, func=ACT.Identity, bias=bias_ap, scale=scale_ap)
-            share = len(postponed) // PASSES
-            for arguments in postponed[g * share : (g + 1) * share]:
-                quantise(*arguments)
             grouped = grouped_pool.tile([P, BLOCK, PACK], BF16, align_bytes=64)
             nc.vector.tensor_copy(out=grouped[:], in_=h_planes[:, g, :, :].rearrange("p t n -> p n t"))
             quantise(grouped, h_codes[:, g, :], h_scales[:, g, :])

from contextlib import ExitStack

import concourse.mybir as mybir
from concourse.masks import make_identity

F32 = mybir.dt.float32
BF16 = mybir.dt.bfloat16
U32 = mybir.dt.uint32
U8 = mybir.dt.uint8
FP8X4 = mybir.dt.float8_e4m3fn_x4
ACT = mybir.ActivationFunctionType
ALU = mybir.AluOpType

P = 128
PACK = 4
K = 2048
PASSES = K // (P * PACK)
TOKENS = 256
TOKEN_TILES = TOKENS // P
D_MODEL = 2048
D_FF = 4096
BLOCK = 256
GROUP = 512
GROUPS_OUT = D_MODEL // GROUP
GROUPS = GROUPS_OUT + D_FF // GROUP
EPS = 1e-5

RAW_BUFS = 10

FLOPS = 2 * TOKENS * K * (D_MODEL + D_FF)


def tile_minitransformerlayer_pb_kernel(tc, h_attn, x, w_out, w_fc1, g2, b2, out_0, out_1):
    nc = tc.nc
    x_rows = x.flatten_outer_dims()
    x_mid_rows = out_0.flatten_outer_dims()
    act_rows = out_1.flatten_outer_dims()

    blocks = [h_attn.flatten_outer_dims()]
    blocks.extend([w_out[r : r + BLOCK, :] for r in range(0, D_MODEL, BLOCK)])
    blocks.extend([w_fc1[r : r + BLOCK, :] for r in range(0, D_FF, BLOCK)])

    with ExitStack() as ctx:
        ctx.enter_context(tc.manual_schedule())
        const = ctx.enter_context(tc.tile_pool(name="const", bufs=1))
        raw_pool = ctx.enter_context(tc.tile_pool(name="raw", bufs=RAW_BUFS))
        grouped_pool = ctx.enter_context(tc.tile_pool(name="grouped", bufs=8))
        weight_pool = ctx.enter_context(tc.tile_pool(name="weights", bufs=4))
        result_pool = ctx.enter_context(tc.tile_pool(name="result", bufs=8))
        bank_pool = ctx.enter_context(tc.psum_pool(name="banks", bufs=6))
        acc_pool = ctx.enter_context(tc.psum_pool(name="acc", bufs=2))

        zero = const.tile([P, 1], F32)
        nc.vector.memset(zero[:], 0.0)
        table_warmer = const.tile([P, 1], F32)
        nc.scalar.activation(out=table_warmer[:], in_=zero[:], func=ACT.Gelu)

        ident = const.tile([P, P], F32)
        make_identity(nc, ident[:])
        minus_half = const.tile([P, TOKEN_TILES], F32)
        nc.gpsimd.memset(minus_half[:], -0.5)

        loaded = []

        def load_next_block():
            if len(loaded) < len(blocks):
                raw = raw_pool.tile([P, 2, K], BF16)
                rows = blocks[len(loaded)]
                nc.sync.dma_start(out=raw[:], in_=rows.rearrange("(p c) k -> p c k", c=2))
                loaded.append(raw)

        gain_rows = const.tile([P, 2 * P], BF16)
        nc.vector.memset(gain_rows[:], 0.0)
        nc.scalar.dma_start(out=gain_rows[0:8, :], in_=g2.rearrange("(r c) -> r c", c=2 * P))
        nc.scalar.dma_start(out=gain_rows[8:16, :], in_=b2.rearrange("(r c) -> r c", c=2 * P))

        x_sb = const.tile([P, TOKEN_TILES, D_MODEL], BF16)
        for b in range(RAW_BUFS):
            load_next_block()
            if b == 4:
                nc.sync.dma_start(out=x_sb[:], in_=x_rows.rearrange("(t p) d -> p t d", p=P))

        def quantise(grouped, codes, scales):
            nc.vector.quantize_mx(
                out=codes.bitcast(FP8X4),
                scales=scales,
                in_=grouped[:].rearrange("p n t -> p (n t)"),
            )

        def pack_block(b, codes, scales, vector_every):
            words = loaded[b][:].bitcast(F32)
            waiting = None
            for g in range(PASSES):
                bank = bank_pool.tile([P, 2, 2, P], F32)
                for u in range(2):
                    first = (2 * g + u) * P
                    for c in range(2):
                        nc.tensor.transpose(bank[:, u, c, :], words[:, c, first : first + P], ident[:])
                grouped = grouped_pool.tile([P, BLOCK, PACK], BF16, align_bytes=64)
                to_words = grouped[:].bitcast(F32).rearrange("p (j c) u -> p j c u", c=2)
                from_bank = bank[:].rearrange("p u c j -> p j c u")
                bank_number = b * PASSES + g
                if vector_every and bank_number % vector_every == vector_every - 1:
                    nc.vector.tensor_copy(out=to_words, in_=from_bank)
                else:
                    nc.scalar.copy(out=to_words, in_=from_bank)
                if waiting is not None:
                    quantise(*waiting)
                waiting = (grouped, codes[:, g, :], scales[:, g, :])
            quantise(*waiting)
            load_next_block()

        def prepare_group(i):
            if i < GROUPS_OUT:
                vector_every = 4
            elif i == GROUPS_OUT:
                vector_every = 0
            else:
                vector_every = 3
            codes = weight_pool.tile([P, PASSES, GROUP], U32, align_bytes=64)
            scales = weight_pool.tile([P, PASSES, GROUP], U8, align_bytes=64)
            for half in range(2):
                cols = slice(half * BLOCK, (half + 1) * BLOCK)
                pack_block(1 + 2 * i + half, codes[:, :, cols], scales[:, :, cols], vector_every)
            return codes, scales

        def mx_product(tokens, weights, tt):
            token_codes, token_scales = tokens
            weight_codes, weight_scales = weights
            rows = slice(tt * P, (tt + 1) * P)
            acc = acc_pool.tile([P, GROUP], F32)
            for g in range(PASSES):
                nc.tensor.matmul_mx(
                    out=acc[:],
                    lhsT=token_codes[:, g, rows].bitcast(FP8X4),
                    lhsT_scale=token_scales[:, g, rows],
                    rhs=weight_codes[:, g, :].bitcast(FP8X4),
                    rhs_scale=weight_scales[:, g, :],
                    start=(g == 0),
                    stop=(g == PASSES - 1),
                )
            return acc

        attn_codes = const.tile([P, PASSES, TOKENS], U32, align_bytes=64)
        attn_scales = const.tile([P, PASSES, TOKENS], U8, align_bytes=64)
        x_mid = const.tile([P, TOKEN_TILES, D_MODEL], F32)
        stats = const.tile([P, TOKEN_TILES, GROUPS_OUT, 6], F32)

        def project_group(i, weights):
            cols = slice(i * GROUP, (i + 1) * GROUP)
            for tt in range(TOKEN_TILES):
                acc = mx_product((attn_codes, attn_scales), weights, tt)
                nc.vector.tensor_tensor(out=x_mid[:, tt, cols], in0=acc[:], in1=x_sb[:, tt, cols], op=ALU.add)
                nc.vector.bn_stats(out=stats[:, tt, i, :], in_=x_mid[:, tt, cols])

        pack_block(0, attn_codes[:], attn_scales[:], 2)

        bank = bank_pool.tile([P, 2, 2, P], F32)
        nc.tensor.transpose(bank[:, 0, 0, :], gain_rows[:].bitcast(F32), ident[:])
        gain_words = const.tile([P, 16], F32)
        nc.vector.tensor_copy(out=gain_words[:], in_=bank[:, 0, 0, 0:16])
        gain_bias = const.tile([P, 16, 2], F32)
        nc.vector.tensor_copy(out=gain_bias[:], in_=gain_words[:].bitcast(BF16).rearrange("p (r e) -> p r e", e=2))
        gain = gain_bias[:, 0:8, :]
        bias = gain_bias[:, 8:16, :]

        prepared = {0: prepare_group(0)}
        for i in range(1, GROUPS_OUT):
            prepared[i] = prepare_group(i)
            project_group(i - 1, prepared[i - 1])
        project_group(GROUPS_OUT - 1, prepared[GROUPS_OUT - 1])
        for tt in range(TOKEN_TILES):
            nc.sync.dma_start(out=x_mid_rows[tt * P : (tt + 1) * P, :], in_=x_mid[:, tt, :])

        mean_var = const.tile([P, TOKEN_TILES, 2], F32)
        for tt in range(TOKEN_TILES):
            nc.vector.bn_aggr(out=mean_var[:, tt, :], in_=stats[:, tt, :, :].rearrange("p i s -> p (i s)"))
        var_eps = const.tile([P, TOKEN_TILES], F32)
        nc.vector.tensor_scalar_add(out=var_eps[:], in0=mean_var[:, :, 1], scalar1=EPS)
        rstd = const.tile([P, TOKEN_TILES], F32)
        nc.gpsimd.tensor_tensor(out=rstd[:], in0=var_eps[:], in1=minus_half[:], op=ALU.pow)
        z = const.tile([P, TOKEN_TILES, D_MODEL], F32)
        for g in range(PASSES):
            cols = slice(g * P * PACK, (g + 1) * P * PACK)
            for tt in range(TOKEN_TILES):
                nc.vector.tensor_scalar(
                    out=z[:, tt, cols],
                    in0=x_mid[:, tt, cols],
                    scalar1=mean_var[:, tt, 0:1],
                    scalar2=rstd[:, tt : tt + 1],
                    op0=ALU.subtract,
                    op1=ALU.mult,
                )

        prepared[GROUPS_OUT] = prepare_group(GROUPS_OUT)

        h_codes = const.tile([P, PASSES, TOKENS], U32, align_bytes=64)
        h_scales = const.tile([P, PASSES, TOKENS], U8, align_bytes=64)
        h_planes = const.tile([P, PASSES, PACK, TOKENS], BF16)
        z_by_parity = z[:].rearrange("p t (q e) -> p t e q", e=2)
        for g in range(PASSES):
            for u in range(2):
                bank = bank_pool.tile([P, 2, 2, P], F32)
                first = (2 * g + u) * P
                for e in range(2):
                    for tt in range(TOKEN_TILES):
                        nc.tensor.transpose(bank[:, e, tt, :], z_by_parity[:, tt, e, first : first + P], ident[:])
                for e in range(2):
                    plane = h_planes[:, g, 2 * u + e, :]
                    z_t = bank[:, e, :, :].rearrange("p t j -> p (t j)")
                    scale_ap = gain[:, 2 * g + u, e : e + 1]
                    bias_ap = bias[:, 2 * g + u, e : e + 1]
                    nc.scalar.activation(out=plane, in_=z_t, func=ACT.Identity, bias=bias_ap, scale=scale_ap)
            grouped = grouped_pool.tile([P, BLOCK, PACK], BF16, align_bytes=64)
            nc.vector.tensor_copy(out=grouped[:], in_=h_planes[:, g, :, :].rearrange("p t n -> p n t"))
            quantise(grouped, h_codes[:, g, :], h_scales[:, g, :])

        def mlp_group(i, weights):
            cols = slice((i - GROUPS_OUT) * GROUP, (i - GROUPS_OUT + 1) * GROUP)
            for tt in range(TOKEN_TILES):
                acc = mx_product((h_codes, h_scales), weights, tt)
                result = result_pool.tile([P, GROUP], F32)
                nc.scalar.activation(out=result[:], in_=acc[:], func=ACT.Gelu)
                nc.sync.dma_start(out=act_rows[tt * P : (tt + 1) * P, cols], in_=result[:])

        for i in range(GROUPS_OUT + 1, GROUPS):
            prepared[i] = prepare_group(i)
            mlp_group(i - 1, prepared[i - 1])
        mlp_group(GROUPS - 1, prepared[GROUPS - 1])
